import numpy as np
import ml_dtypes


def mxq(x, axis, fmt="e4m3"):
    dtype, down = {"e4m3": (ml_dtypes.float8_e4m3fn, 7), "e5m2": (ml_dtypes.float8_e5m2, 14)}[fmt]
    v = np.moveaxis(np.asarray(x, np.float32).astype(ml_dtypes.bfloat16).astype(np.float64), axis, -1)
    blocks = v.reshape(v.shape[:-1] + (-1, 32))
    amax = np.abs(blocks).max(-1, keepdims=True)
    byte = np.maximum(np.where(amax > 0, np.frexp(amax)[1] - 1 + 127, 0) - down, 1)
    scale = np.exp2(byte - 127.0)
    codes = (blocks / scale).astype(np.float32).astype(dtype).astype(np.float64)
    return np.moveaxis((codes * scale).reshape(v.shape), -1, axis)


WIDE = False


def mx_kscale(k):
    if not WIDE:
        return np.ones(k)
    levels = np.array([10, -10, 5, -5, 0])
    a = np.random.permutation(np.resize(levels, k // 512 * 4)).reshape(k // 512, 4)
    idx = np.arange(k)
    return np.exp2(a[idx // 512, idx % 128 // 32])


BF16 = ml_dtypes.bfloat16


def bf(x):
    return np.asarray(x, np.float32).astype(BF16)


def f64(x):
    return np.asarray(x).astype(np.float64)


E2M1 = np.array([0.0, 0.5, 1.0, 1.5, 2.0, 3.0, 4.0, 6.0, -0.0, -0.5, -1.0, -1.5, -2.0, -3.0, -4.0, -6.0])


def pack_weight(w, fmt):
    k, n = w.shape
    w = f64(bf(w)).reshape(k // 32, 32, n)
    amax = np.abs(w).max(1)
    if fmt == "e4m3":
        byte = np.frexp(amax)[1] - 1 + 127 - 7
    else:
        mant, ex = np.frexp(amax / 6.0)
        byte = np.where(mant > 0.5, ex, ex - 1) + 127
    byte = np.clip(np.where(amax > 0, byte, 1), 1, 254)
    scaled = (w * np.exp2(127.0 - byte)[:, None, :]).reshape(k, n).astype(np.float32)
    by_word = np.ascontiguousarray(scaled.reshape(k // 512, 128, 4, n).transpose(0, 1, 3, 2))
    if fmt == "e4m3":
        words = by_word.astype(ml_dtypes.float8_e4m3fn).view(np.uint8)
    else:
        c = by_word.astype(ml_dtypes.float4_e2m1fn).view(np.uint8) & 0xF
        words = c[..., 0::2] | (c[..., 1::2] << 4)
    return np.ascontiguousarray(words), np.ascontiguousarray(byte.astype(np.uint8).reshape(k // 512, 16, n))


def unpack_weight(words, scales, fmt):
    g, p, n, _ = words.shape
    if fmt == "e4m3":
        vals = np.ascontiguousarray(words).view(ml_dtypes.float8_e4m3fn).astype(np.float64)
    else:
        nib = np.empty((g, p, n, 4), np.uint8)
        nib[..., 0::2] = words & 0xF
        nib[..., 1::2] = words >> 4
        vals = E2M1[nib]
    vals = vals * np.repeat(np.exp2(scales.astype(np.float64) - 127.0), 8, axis=1)[..., None]
    return vals.transpose(0, 1, 3, 2).reshape(g * 512, n)


B, D, E, H, L = 4096, 512, 4, 512, 128
NOISE_EPS = 0.01
MEAN_EPS = 1e-8
FMT = "e4m3"


def softplus(z):
    return np.log(1.0 + np.exp(z))


def noisy_gates(clean_logits, noise_pre, noise):
    sd = softplus(noise_pre) + NOISE_EPS
    l = clean_logits + noise * sd
    e = np.exp(l - l.max(1, keepdims=True))
    p = e / e.sum(1, keepdims=True)
    m = p.mean(-1) - MEAN_EPS
    g = np.where(p >= m[:, None], p, 0.0)
    return g / g.sum(-1, keepdims=True)


def setup_inputs():
    s = mx_kscale(D)
    x = bf(np.random.standard_normal((B, D)) * s)
    noise = bf(np.random.standard_normal((B, E)))
    clean_logits = bf(np.random.standard_normal((B, E)))
    noise_pre = bf(np.random.standard_normal((B, E)))
    W1 = np.random.standard_normal((E, D, H)) / np.sqrt(D) / s[None, :, None]
    b1 = bf(np.random.standard_normal((E, H)) * 0.2)
    W2 = np.random.standard_normal((E, H, L)) * 2.0 / np.sqrt(H)
    b2 = bf(np.random.standard_normal((E, L)) * 0.3)
    W1_words, W1_scales = pack_weight(W1.reshape(-1, H), FMT)
    W2_words, W2_scales = pack_weight(W2.reshape(-1, L), FMT)
    return {"x": x,
            "noise": noise,
            "clean_logits": clean_logits,
            "noise_pre": noise_pre,
            "W1_words": W1_words,
            "W1_scales": W1_scales,
            "b1": b1,
            "W2_words": W2_words,
            "W2_scales": W2_scales,
            "b2": b2}


def reference(x, noise, clean_logits, noise_pre, W1_words, W1_scales, b1, W2_words, W2_scales, b2):
    gates = noisy_gates(f64(clean_logits), f64(noise_pre), f64(noise))
    h = np.tanh((mxq(f64(x), 1, "e4m3") @ unpack_weight(W1_words, W1_scales, FMT).reshape(E, D, H)) + f64(b1)[:, None, :])
    y = (mxq(h, 2, "e4m3") @ unpack_weight(W2_words, W2_scales, FMT).reshape(E, H, L)) + f64(b2)[:, None, :]
    return gates[:, :, None] * y.transpose(1, 0, 2)

@@ -1,0 +1,289 @@
+from contextlib import ExitStack
+
+import concourse.mybir as mybir
+from concourse.masks import make_identity
+
+FP8X4 = mybir.dt.float8_e4m3fn_x4
+BF16 = mybir.dt.bfloat16
+F32 = mybir.dt.float32
+I32 = mybir.dt.int32
+U32 = mybir.dt.uint32
+U8 = mybir.dt.uint8
+ACT = mybir.ActivationFunctionType
+ALU = mybir.AluOpType
+AX = mybir.AxisListType
+
+P = 128
+PACK = 4
+B, D, E, H, L = 4096, 512, 4, 512, 128
+TILES = B // P
+CHUNK = 4
+CHUNKS = TILES // CHUNK
+UNITS = TILES * E
+PAIRS = UNITS // 2
+NOISE_EPS = 0.01
+MEAN_EPS = 1e-8
+
+FLOPS = 2 * B * E * (D * H + H * L)
+
+
+def tile_mblfe_pa_t_e_kernel(
+    tc, x, noise, clean_logits, noise_pre, W1_words, W1_scales, b1, W2_words, W2_scales, b2, out
+):
+    nc = tc.nc
+    with ExitStack() as ctx:
+        keep = ctx.enter_context(tc.tile_pool(name="keep", bufs=1))
+        xin = ctx.enter_context(tc.tile_pool(name="xin", bufs=CHUNKS))
+        xgr = ctx.enter_context(tc.tile_pool(name="xgr", bufs=2))
+        zbp = ctx.enter_context(tc.tile_pool(name="zbp", bufs=6))
+        hgr = ctx.enter_context(tc.tile_pool(name="hgr", bufs=3))
+        hq = ctx.enter_context(tc.tile_pool(name="hq", bufs=3))
+        ybp = ctx.enter_context(tc.tile_pool(name="ybp", bufs=2))
+        obp = ctx.enter_context(tc.tile_pool(name="obp", bufs=3))
+        zps = ctx.enter_context(tc.psum_pool(name="zps", bufs=4))
+        trp = ctx.enter_context(tc.psum_pool(name="trp", bufs=3))
+        yps = ctx.enter_context(tc.psum_pool(name="yps", bufs=1))
+
+        x_rows = x.rearrange("(p i) d -> p i d", i=TILES)
+        out_rows = out.rearrange("(p i) e l -> p i (e l)", i=TILES)
+
+        w1_words = keep.tile([P, E, H], U32, align_bytes=64)
+        w1_planes = keep.tile([P, H], U8, align_bytes=64)
+        w2_words = keep.tile([P, E, L], U32, align_bytes=64)
+        w2_planes = keep.tile([P, L], U8, align_bytes=64)
+        nc.vector.memset(w1_planes[:].bitcast(I32), 0)
+        nc.vector.memset(w2_planes[:].bitcast(I32), 0)
+
+        x_chunks = []
+        for c in range(CHUNKS):
+            x_chunk = xin.tile([P, CHUNK, D], BF16, name="x_chunk")
+            x_chunks.append(x_chunk)
+
+        def load_x(c):
+            nc.sync.dma_start(out=x_chunks[c][:], in_=x_rows[:, CHUNK * c : CHUNK * (c + 1), :])
+
+        def load_planes(planes, scales):
+            for quad in range(4):
+                nc.sync.dma_start(
+                    out=planes[32 * quad : 32 * quad + 16, :].bitcast(I32),
+                    in_=scales[:, 4 * quad : 4 * quad + 4, :].bitcast(I32),
+                )
+
+        load_x(0)
+        load_planes(w1_planes, W1_scales)
+        for e in range(E):
+            nc.sync.dma_start(
+                out=w1_words[:, e, :].bitcast(I32),
+                in_=W1_words[e].rearrange("p n t -> p (n t)").bitcast(I32),
+            )
+        load_x(1)
+        load_planes(w2_planes, W2_scales)
+        for e in range(E):
+            nc.sync.dma_start(
+                out=w2_words[:, e, :].bitcast(I32),
+                in_=W2_words[e].rearrange("p n t -> p (n t)").bitcast(I32),
+            )
+        for c in range(2, CHUNKS):
+            load_x(c)
+
+        b1_rows = keep.tile([P, E * H], BF16)
+        nc.scalar.dma_start(out=b1_rows[:], in_=b1.rearrange("e h -> (e h)").partition_broadcast(P))
+        pre_in = keep.tile([P, TILES * E], BF16)
+        nc.scalar.dma_start(out=pre_in[:], in_=noise_pre.rearrange("(p i) e -> p (i e)", i=TILES))
+        noise_in = keep.tile([P, TILES * E], BF16)
+        nc.scalar.dma_start(out=noise_in[:], in_=noise.rearrange("(p i) e -> p (i e)", i=TILES))
+        clean_in = keep.tile([P, TILES * E], BF16)
+        nc.scalar.dma_start(out=clean_in[:], in_=clean_logits.rearrange("(p i) e -> p (i e)", i=TILES))
+        b2_rows = keep.tile([P, E, L], BF16)
+        nc.scalar.dma_start(
+            out=b2_rows[:].rearrange("p e l -> p (e l)"),
+            in_=b2.rearrange("e l -> (e l)").partition_broadcast(P),
+        )
+
+        ident = keep.tile([P, P], F32)
+        make_identity(nc, ident[:])
+
+        b1_sorted = keep.tile([P, E, PACK, H // PACK], F32)
+        nc.vector.tensor_copy(
+            out=b1_sorted[:], in_=b1_rows[:].rearrange("p (e q t) -> p e t q", e=E, t=PACK)
+        )
+
+        x_words = keep.tile([P, TILES * P], U32, align_bytes=64)
+        x_planes = keep.tile([P, TILES * P], U8, align_bytes=64)
+        x_groups = {}
+
+        def transpose_x(c):
+            grouped = xgr.tile([P, CHUNK, P, PACK], BF16, align_bytes=64, name="x_grouped")
+            x_groups[c] = grouped
+            grouped_words = grouped[:].bitcast(F32)
+            for half in range(CHUNK // 2):
+                turned = trp.tile([P, 2, 2, P], F32, tag="turned", name="x_turned")
+                for j in range(2):
+                    row_words = x_chunks[c][:, 2 * half + j, :].bitcast(F32)
+                    for u in range(2):
+                        nc.tensor.transpose(turned[:, j, u, :], row_words[:, u : D // 2 : 2], ident[:])
+                nc.scalar.copy(
+                    out=grouped_words[:, 2 * half : 2 * half + 2, :, :],
+                    in_=turned[:].rearrange("q j u b -> q j b u"),
+                )
+
+        def quantise_x(c):
+            cols = slice(CHUNK * P * c, CHUNK * P * (c + 1))
+            nc.vector.quantize_mx(
+                out=x_words[:, cols].bitcast(FP8X4),
+                scales=x_planes[:, cols],
+                in_=x_groups[c][:].rearrange("q j b t -> q (j b t)"),
+            )
+
+        def small(name, width=TILES * E):
+            return keep.tile([P, width], F32, name=name)
+
+        def by_expert(t):
+            return t[:].rearrange("p (i e) -> p i e", e=E)
+
+        def over_experts(t):
+            return t[:].unsqueeze(2).to_broadcast([P, TILES, E])
+
+        gates = small("gates")
+
+        def compute_gates():
+            mag = small("mag")
+            nc.scalar.activation(out=mag[:], in_=pre_in[:], func=ACT.Abs)
+            nc.scalar.activation(out=mag[:], in_=mag[:], func=ACT.Exp, scale=-1.0)
+            nc.scalar.activation(out=mag[:], in_=mag[:], func=ACT.Ln, bias=1.0)
+            pos = small("pos")
+            nc.vector.tensor_scalar_max(out=pos[:], in0=pre_in[:], scalar1=0.0)
+            logit = small("logit")
+            nc.vector.scalar_tensor_tensor(
+                out=logit[:], in0=mag[:], scalar=NOISE_EPS, in1=pos[:], op0=ALU.add, op1=ALU.add
+            )
+            nc.vector.tensor_tensor(out=logit[:], in0=logit[:], in1=noise_in[:], op=ALU.mult)
+            nc.vector.tensor_tensor(out=logit[:], in0=logit[:], in1=clean_in[:], op=ALU.add)
+            top = small("top", TILES)
+            nc.vector.tensor_reduce(out=top[:], in_=by_expert(logit), axis=AX.X, op=ALU.max)
+            nc.vector.tensor_tensor(
+                out=by_expert(logit), in0=by_expert(logit), in1=over_experts(top), op=ALU.subtract
+            )
+            prob = small("prob")
+            nc.scalar.activation(out=prob[:], in_=logit[:], func=ACT.Exp)
+            total = small("total", TILES)
+            nc.vector.tensor_reduce(out=total[:], in_=by_expert(prob), axis=AX.X, op=ALU.add)
+            nc.vector.reciprocal(out=total[:], in_=total[:])
+            nc.vector.tensor_tensor(
+                out=by_expert(prob), in0=by_expert(prob), in1=over_experts(total), op=ALU.mult
+            )
+            cut = small("cut", TILES)
+            nc.vector.tensor_reduce(out=cut[:], in_=by_expert(prob), axis=AX.X, op=ALU.add)
+            nc.vector.tensor_scalar(
+                out=cut[:], in0=cut[:], scalar1=1.0 / E, scalar2=MEAN_EPS, op0=ALU.mult, op1=ALU.subtract
+            )
+            kept = small("kept")
+            nc.vector.tensor_tensor(
+                out=by_expert(kept), in0=by_expert(prob), in1=over_experts(cut), op=ALU.is_ge
+            )
+            nc.vector.tensor_tensor(out=kept[:], in0=kept[:], in1=prob[:], op=ALU.mult)
+            kept_sum = small("kept_sum", TILES)
+            nc.vector.tensor_reduce(out=kept_sum[:], in_=by_expert(kept), axis=AX.X, op=ALU.add)
+            nc.vector.reciprocal(out=kept_sum[:], in_=kept_sum[:])
+            nc.vector.tensor_tensor(
+                out=by_expert(gates), in0=by_expert(kept), in1=over_experts(kept_sum), op=ALU.mult
+            )
+
+        biased = {}
+        h_groups = {}
+        h_packed = {}
+        y_banks = {}
+        out_tiles = {}
+
+        def first_matmul(u):
+            i, e = divmod(u, E)
+            z = zps.tile([P, H], F32, name="z")
+            nc.tensor.matmul_mx(
+                out=z[:],
+                lhsT=x_words[:, P * i : P * (i + 1)].bitcast(FP8X4),
+                lhsT_scale=x_planes[:, P * i : P * (i + 1)],
+                rhs=w1_words[:, e, :].bitcast(FP8X4),
+                rhs_scale=w1_planes[4 * e : P, :],
+                start=True,
+                stop=True,
+            )
+            zb = zbp.tile([P, PACK, H // PACK], F32, name="zb")
+            biased[u] = zb
+            nc.vector.tensor_tensor(
+                out=zb[:], in0=z[:].rearrange("b (q t) -> b t q", t=PACK), in1=b1_sorted[:, e], op=ALU.add
+            )
+
+        def turn_and_tanh(u):
+            i, e = divmod(u, E)
+            if e == 0:
+                h_grouped = hgr.tile([P, E, P, PACK], BF16, align_bytes=64, name="h_grouped")
+                h_groups[i] = h_grouped
+            turned = trp.tile([P, PACK, P], F32, tag="turned", name="z_turned")
+            for t in range(PACK):
+                nc.tensor.transpose(turned[:, t, :], biased[u][:, t, :], ident[:])
+            nc.scalar.activation(
+                out=h_groups[i][:, e, :, :], in_=turned[:].rearrange("q t b -> q b t"), func=ACT.Tanh
+            )
+
+        def second_matmul(i):
+            words = hq.tile([P, E * P], U32, align_bytes=64, name="h_words")
+            planes = hq.tile([P, E * P], U8, align_bytes=64, name="h_planes")
+            nc.vector.quantize_mx(
+                out=words[:].bitcast(FP8X4),
+                scales=planes[:],
+                in_=h_groups[i][:].rearrange("q e b t -> q (e b t)"),
+            )
+            y = yps.tile([P, E, L], F32, name="y")
+            y_banks[i] = y
+            for e in range(E):
+                nc.tensor.matmul_mx(
+                    out=y[:, e, :],
+                    lhsT=words[:, P * e : P * (e + 1)].bitcast(FP8X4),
+                    lhsT_scale=planes[:, P * e : P * (e + 1)],
+                    rhs=w2_words[:, e, :].bitcast(FP8X4),
+                    rhs_scale=w2_planes[4 * e : P, :],
+                    start=True,
+                    stop=True,
+                )
+
+        def finish(i):
+            c, j = divmod(i, CHUNK)
+            if j == 0:
+                out_tile = obp.tile([P, CHUNK, E, L], F32, name="out_tile")
+                out_tiles[c] = out_tile
+            yb = ybp.tile([P, E, L], F32, name="yb")
+            nc.vector.tensor_tensor(out=yb[:], in0=y_banks[i][:], in1=b2_rows[:], op=ALU.add)
+            for e in range(E):
+                nc.scalar.activation(
+                    out=out_tiles[c][:, j, e, :],
+                    in_=yb[:, e, :],
+                    func=ACT.Copy,
+                    scale=gates[:, E * i + e : E * i + e + 1],
+                )
+            if j == CHUNK - 1:
+                nc.sync.dma_start(
+                    out=out_rows[:, CHUNK * c : CHUNK * (c + 1), :],
+                    in_=out_tiles[c][:].rearrange("p j e l -> p j (e l)"),
+                )
+
+        transpose_x(0)
+        quantise_x(0)
+        compute_gates()
+
+        pairs_per_chunk = PAIRS // CHUNKS
+        for k in range(PAIRS + 4):
+            if k < PAIRS:
+                first_matmul(2 * k)
+                first_matmul(2 * k + 1)
+            if k >= 3 and k % 2 == 1 and (k - 3) // 2 < TILES:
+                second_matmul((k - 3) // 2)
+            if k >= 4 and k % 2 == 0 and (k - 4) // 2 < TILES:
+                finish((k - 4) // 2)
+            if 1 <= k <= PAIRS:
+                turn_and_tanh(2 * k - 2)
+                turn_and_tanh(2 * k - 1)
+            c_next = k // pairs_per_chunk + 1
+            if c_next < CHUNKS and k % pairs_per_chunk == 2:
+                transpose_x(c_next)
+            if c_next < CHUNKS and k % pairs_per_chunk == 4:
+                quantise_x(c_next)

@@ -19,8 +19,9 @@ B, D, E, H, L = 4096, 512, 4, 512, 128
 TILES = B // P
 CHUNK = 4
 CHUNKS = TILES // CHUNK
-UNITS = TILES * E
-PAIRS = UNITS // 2
+ROWS = CHUNK * P
+ROUNDS = CHUNKS * E
+SETS = H // P
 NOISE_EPS = 0.01
 MEAN_EPS = 1e-8
 
@@ -35,32 +36,32 @@ def tile_mblfe_pa_t_e_kernel(
         keep = ctx.enter_context(tc.tile_pool(name="keep", bufs=1))
         xin = ctx.enter_context(tc.tile_pool(name="xin", bufs=CHUNKS))
         xgr = ctx.enter_context(tc.tile_pool(name="xgr", bufs=2))
-        zbp = ctx.enter_context(tc.tile_pool(name="zbp", bufs=6))
+        htp = ctx.enter_context(tc.tile_pool(name="htp", bufs=12))
+        plp = ctx.enter_context(tc.tile_pool(name="plp", bufs=4))
         hgr = ctx.enter_context(tc.tile_pool(name="hgr", bufs=3))
         hq = ctx.enter_context(tc.tile_pool(name="hq", bufs=3))
         ybp = ctx.enter_context(tc.tile_pool(name="ybp", bufs=2))
         obp = ctx.enter_context(tc.tile_pool(name="obp", bufs=3))
         zps = ctx.enter_context(tc.psum_pool(name="zps", bufs=4))
-        trp = ctx.enter_context(tc.psum_pool(name="trp", bufs=3))
-        yps = ctx.enter_context(tc.psum_pool(name="yps", bufs=1))
+        trp = ctx.enter_context(tc.psum_pool(name="trp", bufs=2))
+        yps = ctx.enter_context(tc.psum_pool(name="yps", bufs=2))
 
         x_rows = x.rearrange("(p i) d -> p i d", i=TILES)
         out_rows = out.rearrange("(p i) e l -> p i (e l)", i=TILES)
 
-        w1_words = keep.tile([P, E, H], U32, align_bytes=64)
-        w1_planes = keep.tile([P, H], U8, align_bytes=64)
+        w1_raw = keep.tile([P, E, H], U32, align_bytes=64)
+        w1_planes_raw = keep.tile([P, H], U8, align_bytes=64)
         w2_words = keep.tile([P, E, L], U32, align_bytes=64)
         w2_planes = keep.tile([P, L], U8, align_bytes=64)
-        nc.vector.memset(w1_planes[:].bitcast(I32), 0)
+        b1_as_rows = keep.tile([P, P], BF16)
+        nc.vector.memset(w1_planes_raw[:].bitcast(I32), 0)
         nc.vector.memset(w2_planes[:].bitcast(I32), 0)
+        nc.vector.memset(b1_as_rows[:], 0.0)
 
         x_chunks = []
         for c in range(CHUNKS):
             x_chunk = xin.tile([P, CHUNK, D], BF16, name="x_chunk")
             x_chunks.append(x_chunk)
-
-        def load_x(c):
-            nc.sync.dma_start(out=x_chunks[c][:], in_=x_rows[:, CHUNK * c : CHUNK * (c + 1), :])
 
         def load_planes(planes, scales):
             for quad in range(4):
@@ -69,25 +70,27 @@ def tile_mblfe_pa_t_e_kernel(
                     in_=scales[:, 4 * quad : 4 * quad + 4, :].bitcast(I32),
                 )
 
-        load_x(0)
-        load_planes(w1_planes, W1_scales)
+        nc.sync.dma_start(out=x_chunks[0][:], in_=x_rows[:, 0:CHUNK, :])
+        load_planes(w1_planes_raw, W1_scales)
         for e in range(E):
             nc.sync.dma_start(
-                out=w1_words[:, e, :].bitcast(I32),
+                out=w1_raw[:, e, :].bitcast(I32),
                 in_=W1_words[e].rearrange("p n t -> p (n t)").bitcast(I32),
             )
-        load_x(1)
         load_planes(w2_planes, W2_scales)
         for e in range(E):
             nc.sync.dma_start(
                 out=w2_words[:, e, :].bitcast(I32),
                 in_=W2_words[e].rearrange("p n t -> p (n t)").bitcast(I32),
             )
-        for c in range(2, CHUNKS):
-            load_x(c)
+        for c in range(1, CHUNKS):
+            nc.gpsimd.dma_start(out=x_chunks[c][:], in_=x_rows[:, CHUNK * c : CHUNK * (c + 1), :])
 
-        b1_rows = keep.tile([P, E * H], BF16)
-        nc.scalar.dma_start(out=b1_rows[:], in_=b1.rearrange("e h -> (e h)").partition_broadcast(P))
+        for e in range(E):
+            nc.scalar.dma_start(
+                out=b1_as_rows[SETS * e : SETS * (e + 1), :].rearrange("s (a i) -> s a i", i=PACK),
+                in_=b1[e].rearrange("(a s i) -> s a i", s=SETS, i=PACK),
+            )
         pre_in = keep.tile([P, TILES * E], BF16)
         nc.scalar.dma_start(out=pre_in[:], in_=noise_pre.rearrange("(p i) e -> p (i e)", i=TILES))
         noise_in = keep.tile([P, TILES * E], BF16)
@@ -103,13 +106,21 @@ def tile_mblfe_pa_t_e_kernel(
         ident = keep.tile([P, P], F32)
         make_identity(nc, ident[:])
 
-        b1_sorted = keep.tile([P, E, PACK, H // PACK], F32)
+        w1_words = keep.tile([P, E, SETS, P], U32, align_bytes=64)
+        w1_planes = keep.tile([P, SETS, P], U8, align_bytes=64)
         nc.vector.tensor_copy(
-            out=b1_sorted[:], in_=b1_rows[:].rearrange("p (e q t) -> p e t q", e=E, t=PACK)
+            out=w1_planes[:].bitcast(I32),
+            in_=w1_planes_raw[:].bitcast(I32).rearrange("p (a s) -> p s a", s=SETS),
         )
 
-        x_words = keep.tile([P, TILES * P], U32, align_bytes=64)
-        x_planes = keep.tile([P, TILES * P], U8, align_bytes=64)
+        def sort_w1(e):
+            nc.vector.tensor_copy(
+                out=w1_words[:, e].bitcast(I32).rearrange("p s (a i) -> p s a i", i=PACK),
+                in_=w1_raw[:, e, :].bitcast(I32).rearrange("p (a s i) -> p s a i", s=SETS, i=PACK),
+            )
+
+        x_words = keep.tile([P, B], U32, align_bytes=64)
+        x_planes = keep.tile([P, B], U8, align_bytes=64)
         x_groups = {}
 
         def transpose_x(c):
@@ -117,7 +128,7 @@ def tile_mblfe_pa_t_e_kernel(
             x_groups[c] = grouped
             grouped_words = grouped[:].bitcast(F32)
             for half in range(CHUNK // 2):
-                turned = trp.tile([P, 2, 2, P], F32, tag="turned", name="x_turned")
+                turned = trp.tile([P, 2, 2, P], F32, name="x_turned")
                 for j in range(2):
                     row_words = x_chunks[c][:, 2 * half + j, :].bitcast(F32)
                     for u in range(2):
@@ -128,12 +139,21 @@ def tile_mblfe_pa_t_e_kernel(
                 )
 
         def quantise_x(c):
-            cols = slice(CHUNK * P * c, CHUNK * P * (c + 1))
+            cols = slice(ROWS * c, ROWS * (c + 1))
             nc.vector.quantize_mx(
                 out=x_words[:, cols].bitcast(FP8X4),
                 scales=x_planes[:, cols],
                 in_=x_groups[c][:].rearrange("q j b t -> q (j b t)"),
             )
+
+        b1_cols = keep.tile([P, P], F32)
+
+        def spread_b1():
+            b1_wide = keep.tile([P, P], F32, name="b1_wide")
+            nc.vector.tensor_copy(out=b1_wide[:], in_=b1_as_rows[:])
+            b1_turned = trp.tile([P, P], F32, name="b1_turned", tag="x_turned")
+            nc.tensor.transpose(b1_turned[:], b1_wide[:], ident[:])
+            nc.vector.tensor_copy(out=b1_cols[:], in_=b1_turned[:])
 
         def small(name, width=TILES * E):
             return keep.tile([P, width], F32, name=name)
@@ -189,101 +209,99 @@ def tile_mblfe_pa_t_e_kernel(
                 out=by_expert(gates), in0=by_expert(kept), in1=over_experts(kept_sum), op=ALU.mult
             )
 
-        biased = {}
-        h_groups = {}
-        h_packed = {}
+        h_planes_of = {}
         y_banks = {}
         out_tiles = {}
 
-        def first_matmul(u):
-            i, e = divmod(u, E)
-            z = zps.tile([P, H], F32, name="z")
-            nc.tensor.matmul_mx(
-                out=z[:],
-                lhsT=x_words[:, P * i : P * (i + 1)].bitcast(FP8X4),
-                lhsT_scale=x_planes[:, P * i : P * (i + 1)],
-                rhs=w1_words[:, e, :].bitcast(FP8X4),
-                rhs_scale=w1_planes[4 * e : P, :],
-                start=True,
-                stop=True,
-            )
-            zb = zbp.tile([P, PACK, H // PACK], F32, name="zb")
-            biased[u] = zb
-            nc.vector.tensor_tensor(
-                out=zb[:], in0=z[:].rearrange("b (q t) -> b t q", t=PACK), in1=b1_sorted[:, e], op=ALU.add
-            )
+        def hidden(r):
+            c, e = divmod(r, E)
+            apart = plp.tile([P, PACK, ROWS], BF16, name="h_apart")
+            h_planes_of[r] = apart
+            for s in range(SETS):
+                z = zps.tile([P, ROWS], F32, name="z")
+                nc.tensor.matmul_mx(
+                    out=z[:],
+                    lhsT=w1_words[:, e, s, :].bitcast(FP8X4),
+                    lhsT_scale=w1_planes[4 * e : P, s, :],
+                    rhs=x_words[:, ROWS * c : ROWS * (c + 1)].bitcast(FP8X4),
+                    rhs_scale=x_planes[:, ROWS * c : ROWS * (c + 1)],
+                    start=True,
+                    stop=True,
+                )
+                h_set = htp.tile([P, ROWS], BF16, name="h_set")
+                col = SETS * e + s
+                nc.scalar.activation(out=h_set[:], in_=z[:], func=ACT.Tanh, bias=b1_cols[:, col : col + 1])
+                nc.sync.dma_start(out=apart[s:P:SETS, :, :], in_=h_set[:])
 
-        def turn_and_tanh(u):
-            i, e = divmod(u, E)
-            if e == 0:
-                h_grouped = hgr.tile([P, E, P, PACK], BF16, align_bytes=64, name="h_grouped")
-                h_groups[i] = h_grouped
-            turned = trp.tile([P, PACK, P], F32, tag="turned", name="z_turned")
-            for t in range(PACK):
-                nc.tensor.transpose(turned[:, t, :], biased[u][:, t, :], ident[:])
-            nc.scalar.activation(
-                out=h_groups[i][:, e, :, :], in_=turned[:].rearrange("q t b -> q b t"), func=ACT.Tanh
+        def second_matmul(r):
+            c, e = divmod(r, E)
+            grouped = hgr.tile([P, ROWS, PACK], BF16, align_bytes=64, name="h_grouped")
+            nc.vector.tensor_copy(
+                out=grouped[:].rearrange("q (g i) t -> q g t i", i=4),
+                in_=h_planes_of[r][:].rearrange("q t (g i) -> q g t i", i=4),
             )
-
-        def second_matmul(i):
-            words = hq.tile([P, E * P], U32, align_bytes=64, name="h_words")
-            planes = hq.tile([P, E * P], U8, align_bytes=64, name="h_planes")
+            words = hq.tile([P, ROWS], U32, align_bytes=64, name="h_words")
+            planes = hq.tile([P, ROWS], U8, align_bytes=64, name="h_planes")
             nc.vector.quantize_mx(
                 out=words[:].bitcast(FP8X4),
                 scales=planes[:],
-                in_=h_groups[i][:].rearrange("q e b t -> q (e b t)"),
+                in_=grouped[:].rearrange("q b t -> q (b t)"),
             )
-            y = yps.tile([P, E, L], F32, name="y")
-            y_banks[i] = y
-            for e in range(E):
+            y = yps.tile([P, CHUNK, L], F32, name="y")
+            y_banks[r] = y
+            for j in range(CHUNK):
                 nc.tensor.matmul_mx(
-                    out=y[:, e, :],
-                    lhsT=words[:, P * e : P * (e + 1)].bitcast(FP8X4),
-                    lhsT_scale=planes[:, P * e : P * (e + 1)],
+                    out=y[:, j, :],
+                    lhsT=words[:, P * j : P * (j + 1)].bitcast(FP8X4),
+                    lhsT_scale=planes[:, P * j : P * (j + 1)],
                     rhs=w2_words[:, e, :].bitcast(FP8X4),
                     rhs_scale=w2_planes[4 * e : P, :],
                     start=True,
                     stop=True,
                 )
 
-        def finish(i):
-            c, j = divmod(i, CHUNK)
-            if j == 0:
+        def finish(r):
+            c, e = divmod(r, E)
+            if e == 0:
                 out_tile = obp.tile([P, CHUNK, E, L], F32, name="out_tile")
                 out_tiles[c] = out_tile
-            yb = ybp.tile([P, E, L], F32, name="yb")
-            nc.vector.tensor_tensor(out=yb[:], in0=y_banks[i][:], in1=b2_rows[:], op=ALU.add)
-            for e in range(E):
-                nc.scalar.activation(
-                    out=out_tiles[c][:, j, e, :],
-                    in_=yb[:, e, :],
-                    func=ACT.Copy,
-                    scale=gates[:, E * i + e : E * i + e + 1],
-                )
-            if j == CHUNK - 1:
-                nc.sync.dma_start(
+            yb = ybp.tile([P, CHUNK, L], F32, name="yb")
+            nc.vector.tensor_tensor(
+                out=yb[:],
+                in0=y_banks[r][:],
+                in1=b2_rows[:, e, :].unsqueeze(1).to_broadcast([P, CHUNK, L]),
+                op=ALU.add,
+            )
+            nc.vector.tensor_tensor(
+                out=out_tiles[c][:, :, e, :],
+                in0=yb[:],
+                in1=by_expert(gates)[:, CHUNK * c : CHUNK * (c + 1), e].unsqueeze(2).to_broadcast([P, CHUNK, L]),
+                op=ALU.mult,
+            )
+            if e == E - 1:
+                queue = nc.sync if c == CHUNKS - 1 else nc.gpsimd
+                queue.dma_start(
                     out=out_rows[:, CHUNK * c : CHUNK * (c + 1), :],
                     in_=out_tiles[c][:].rearrange("p j e l -> p j (e l)"),
                 )
 
         transpose_x(0)
+        spread_b1()
+        sort_w1(0)
         quantise_x(0)
+        for e in range(1, E):
+            sort_w1(e)
         compute_gates()
 
-        pairs_per_chunk = PAIRS // CHUNKS
-        for k in range(PAIRS + 4):
-            if k < PAIRS:
-                first_matmul(2 * k)
-                first_matmul(2 * k + 1)
-            if k >= 3 and k % 2 == 1 and (k - 3) // 2 < TILES:
-                second_matmul((k - 3) // 2)
-            if k >= 4 and k % 2 == 0 and (k - 4) // 2 < TILES:
-                finish((k - 4) // 2)
-            if 1 <= k <= PAIRS:
-                turn_and_tanh(2 * k - 2)
-                turn_and_tanh(2 * k - 1)
-            c_next = k // pairs_per_chunk + 1
-            if c_next < CHUNKS and k % pairs_per_chunk == 2:
+        for r in range(ROUNDS + 3):
+            if r < ROUNDS:
+                hidden(r)
+            if 2 <= r < ROUNDS + 2:
+                second_matmul(r - 2)
+            if r >= 3:
+                finish(r - 3)
+            c_next = r // E + 1
+            if c_next < CHUNKS and r % E == 0:
                 transpose_x(c_next)
-            if c_next < CHUNKS and k % pairs_per_chunk == 4:
+            if c_next < CHUNKS and r % E == 1:
                 quantise_x(c_next)

@@ -37,7 +37,7 @@ def tile_mblfe_pa_t_e_kernel(
         xin = ctx.enter_context(tc.tile_pool(name="xin", bufs=CHUNKS))
         xgr = ctx.enter_context(tc.tile_pool(name="xgr", bufs=2))
         htp = ctx.enter_context(tc.tile_pool(name="htp", bufs=12))
-        plp = ctx.enter_context(tc.tile_pool(name="plp", bufs=4))
+        plp = ctx.enter_context(tc.tile_pool(name="plp", bufs=6))
         hgr = ctx.enter_context(tc.tile_pool(name="hgr", bufs=3))
         hq = ctx.enter_context(tc.tile_pool(name="hq", bufs=3))
         ybp = ctx.enter_context(tc.tile_pool(name="ybp", bufs=2))
@@ -48,6 +48,9 @@ def tile_mblfe_pa_t_e_kernel(
 
         x_rows = x.rearrange("(p i) d -> p i d", i=TILES)
         out_rows = out.rearrange("(p i) e l -> p i (e l)", i=TILES)
+
+        ident = keep.tile([P, P], F32)
+        make_identity(nc, ident[:])
 
         w1_raw = keep.tile([P, E, H], U32, align_bytes=64)
         w1_planes_raw = keep.tile([P, H], U8, align_bytes=64)
@@ -102,9 +105,6 @@ def tile_mblfe_pa_t_e_kernel(
             out=b2_rows[:].rearrange("p e l -> p (e l)"),
             in_=b2.rearrange("e l -> (e l)").partition_broadcast(P),
         )
-
-        ident = keep.tile([P, P], F32)
-        make_identity(nc, ident[:])
 
         w1_words = keep.tile([P, E, SETS, P], U32, align_bytes=64)
         w1_planes = keep.tile([P, SETS, P], U8, align_bytes=64)
@@ -165,15 +165,15 @@ def tile_mblfe_pa_t_e_kernel(
             return t[:].unsqueeze(2).to_broadcast([P, TILES, E])
 
         gates = small("gates")
+        logit = small("logit")
 
-        def compute_gates():
+        def noisy_logits():
             mag = small("mag")
             nc.scalar.activation(out=mag[:], in_=pre_in[:], func=ACT.Abs)
             nc.scalar.activation(out=mag[:], in_=mag[:], func=ACT.Exp, scale=-1.0)
             nc.scalar.activation(out=mag[:], in_=mag[:], func=ACT.Ln, bias=1.0)
             pos = small("pos")
             nc.vector.tensor_scalar_max(out=pos[:], in0=pre_in[:], scalar1=0.0)
-            logit = small("logit")
             nc.vector.scalar_tensor_tensor(
                 out=logit[:], in0=mag[:], scalar=NOISE_EPS, in1=pos[:], op0=ALU.add, op1=ALU.add
             )
@@ -184,6 +184,8 @@ def tile_mblfe_pa_t_e_kernel(
             nc.vector.tensor_tensor(
                 out=by_expert(logit), in0=by_expert(logit), in1=over_experts(top), op=ALU.subtract
             )
+
+        def gates_from_logits():
             prob = small("prob")
             nc.scalar.activation(out=prob[:], in_=logit[:], func=ACT.Exp)
             total = small("total", TILES)
@@ -210,7 +212,9 @@ def tile_mblfe_pa_t_e_kernel(
             )
 
         h_planes_of = {}
+        h_groups = {}
         y_banks = {}
+        y_biased = {}
         out_tiles = {}
 
         def hidden(r):
@@ -233,13 +237,17 @@ def tile_mblfe_pa_t_e_kernel(
                 nc.scalar.activation(out=h_set[:], in_=z[:], func=ACT.Tanh, bias=b1_cols[:, col : col + 1])
                 nc.sync.dma_start(out=apart[s:P:SETS, :, :], in_=h_set[:])
 
-        def second_matmul(r):
-            c, e = divmod(r, E)
+        def regroup(r):
             grouped = hgr.tile([P, ROWS, PACK], BF16, align_bytes=64, name="h_grouped")
+            h_groups[r] = grouped
             nc.vector.tensor_copy(
                 out=grouped[:].rearrange("q (g i) t -> q g t i", i=4),
                 in_=h_planes_of[r][:].rearrange("q t (g i) -> q g t i", i=4),
             )
+
+        def second_matmul(r):
+            c, e = divmod(r, E)
+            grouped = h_groups[r]
             words = hq.tile([P, ROWS], U32, align_bytes=64, name="h_words")
             planes = hq.tile([P, ROWS], U8, align_bytes=64, name="h_planes")
             nc.vector.quantize_mx(
@@ -260,21 +268,25 @@ def tile_mblfe_pa_t_e_kernel(
                     stop=True,
                 )
 
-        def finish(r):
+        def add_b2(r):
             c, e = divmod(r, E)
-            if e == 0:
-                out_tile = obp.tile([P, CHUNK, E, L], F32, name="out_tile")
-                out_tiles[c] = out_tile
             yb = ybp.tile([P, CHUNK, L], F32, name="yb")
+            y_biased[r] = yb
             nc.vector.tensor_tensor(
                 out=yb[:],
                 in0=y_banks[r][:],
                 in1=b2_rows[:, e, :].unsqueeze(1).to_broadcast([P, CHUNK, L]),
                 op=ALU.add,
             )
+
+        def gate_and_store(r):
+            c, e = divmod(r, E)
+            if e == 0:
+                out_tile = obp.tile([P, CHUNK, E, L], F32, name="out_tile")
+                out_tiles[c] = out_tile
             nc.vector.tensor_tensor(
                 out=out_tiles[c][:, :, e, :],
-                in0=yb[:],
+                in0=y_biased[r][:],
                 in1=by_expert(gates)[:, CHUNK * c : CHUNK * (c + 1), e].unsqueeze(2).to_broadcast([P, CHUNK, L]),
                 op=ALU.mult,
             )
@@ -285,23 +297,30 @@ def tile_mblfe_pa_t_e_kernel(
                     in_=out_tiles[c][:].rearrange("p j e l -> p j (e l)"),
                 )
 
-        transpose_x(0)
-        spread_b1()
-        sort_w1(0)
-        quantise_x(0)
-        for e in range(1, E):
-            sort_w1(e)
-        compute_gates()
+        with tc.manual_schedule():
+            transpose_x(0)
+            spread_b1()
+            sort_w1(0)
+            quantise_x(0)
+            for e in range(1, E):
+                sort_w1(e)
+            noisy_logits()
 
-        for r in range(ROUNDS + 3):
-            if r < ROUNDS:
-                hidden(r)
-            if 2 <= r < ROUNDS + 2:
-                second_matmul(r - 2)
-            if r >= 3:
-                finish(r - 3)
-            c_next = r // E + 1
-            if c_next < CHUNKS and r % E == 0:
-                transpose_x(c_next)
-            if c_next < CHUNKS and r % E == 1:
-                quantise_x(c_next)
+            for r in range(ROUNDS + 6):
+                if r < ROUNDS:
+                    hidden(r)
+                if r == 1:
+                    gates_from_logits()
+                if 0 <= r - 3 < ROUNDS:
+                    regroup(r - 3)
+                if 0 <= r - 5 < ROUNDS:
+                    add_b2(r - 5)
+                if 0 <= r - 4 < ROUNDS:
+                    second_matmul(r - 4)
+                if 0 <= r - 5 < ROUNDS:
+                    gate_and_store(r - 5)
+                c_next = r // E + 1
+                if c_next < CHUNKS and r % E == 0:
+                    transpose_x(c_next)
+                if c_next < CHUNKS and r % E == 1:
+                    quantise_x(c_next)

@@ -22,6 +22,7 @@ CHUNKS = TILES // CHUNK
 ROWS = CHUNK * P
 ROUNDS = CHUNKS * E
 SETS = H // P
+VECTOR_TILES = 3
 NOISE_EPS = 0.01
 MEAN_EPS = 1e-8
 
@@ -35,13 +36,13 @@ def tile_mblfe_pa_t_e_kernel(
     with ExitStack() as ctx:
         keep = ctx.enter_context(tc.tile_pool(name="keep", bufs=1))
         xin = ctx.enter_context(tc.tile_pool(name="xin", bufs=CHUNKS))
-        xgr = ctx.enter_context(tc.tile_pool(name="xgr", bufs=2))
+        xgr = ctx.enter_context(tc.tile_pool(name="xgr", bufs=3))
         htp = ctx.enter_context(tc.tile_pool(name="htp", bufs=12))
         plp = ctx.enter_context(tc.tile_pool(name="plp", bufs=6))
         hgr = ctx.enter_context(tc.tile_pool(name="hgr", bufs=3))
         hq = ctx.enter_context(tc.tile_pool(name="hq", bufs=3))
         ybp = ctx.enter_context(tc.tile_pool(name="ybp", bufs=2))
-        obp = ctx.enter_context(tc.tile_pool(name="obp", bufs=3))
+        obp = ctx.enter_context(tc.tile_pool(name="obp", bufs=4))
         zps = ctx.enter_context(tc.psum_pool(name="zps", bufs=4))
         trp = ctx.enter_context(tc.psum_pool(name="trp", bufs=2))
         yps = ctx.enter_context(tc.psum_pool(name="yps", bufs=2))
@@ -123,27 +124,23 @@ def tile_mblfe_pa_t_e_kernel(
         x_planes = keep.tile([P, B], U8, align_bytes=64)
         x_groups = {}
 
-        def transpose_x(c):
-            grouped = xgr.tile([P, CHUNK, P, PACK], BF16, align_bytes=64, name="x_grouped")
-            x_groups[c] = grouped
-            grouped_words = grouped[:].bitcast(F32)
-            for half in range(CHUNK // 2):
-                turned = trp.tile([P, 2, 2, P], F32, name="x_turned")
-                for j in range(2):
-                    row_words = x_chunks[c][:, 2 * half + j, :].bitcast(F32)
-                    for u in range(2):
-                        nc.tensor.transpose(turned[:, j, u, :], row_words[:, u : D // 2 : 2], ident[:])
-                nc.scalar.copy(
-                    out=grouped_words[:, 2 * half : 2 * half + 2, :, :],
-                    in_=turned[:].rearrange("q j u b -> q j b u"),
-                )
+        def transpose_x(c, half):
+            grouped = xgr.tile([P, 2, P, PACK], BF16, align_bytes=64, name="x_grouped")
+            x_groups[(c, half)] = grouped
+            turned = trp.tile([P, 2, 2, P], F32, name="x_turned")
+            for j in range(2):
+                row_words = x_chunks[c][:, 2 * half + j, :].bitcast(F32)
+                for u in range(2):
+                    nc.tensor.transpose(turned[:, j, u, :], row_words[:, u : D // 2 : 2], ident[:])
+            nc.scalar.copy(out=grouped[:].bitcast(F32), in_=turned[:].rearrange("q j u b -> q j b u"))
 
-        def quantise_x(c):
-            cols = slice(ROWS * c, ROWS * (c + 1))
+        def quantise_x(c, half):
+            first = ROWS * c + 2 * P * half
+            cols = slice(first, first + 2 * P)
             nc.vector.quantize_mx(
                 out=x_words[:, cols].bitcast(FP8X4),
                 scales=x_planes[:, cols],
-                in_=x_groups[c][:].rearrange("q j b t -> q (j b t)"),
+                in_=x_groups[(c, half)][:].rearrange("q j b t -> q (j b t)"),
             )
 
         b1_cols = keep.tile([P, P], F32)
@@ -213,9 +210,9 @@ def tile_mblfe_pa_t_e_kernel(
 
         h_planes_of = {}
         h_groups = {}
+        h_packed = {}
         y_banks = {}
         y_biased = {}
-        out_tiles = {}
 
         def hidden(r):
             c, e = divmod(r, E)
@@ -245,16 +242,19 @@ def tile_mblfe_pa_t_e_kernel(
                 in_=h_planes_of[r][:].rearrange("q t (g i) -> q g t i", i=4),
             )
 
-        def second_matmul(r):
-            c, e = divmod(r, E)
-            grouped = h_groups[r]
+        def quantise_h(r):
             words = hq.tile([P, ROWS], U32, align_bytes=64, name="h_words")
             planes = hq.tile([P, ROWS], U8, align_bytes=64, name="h_planes")
+            h_packed[r] = (words, planes)
             nc.vector.quantize_mx(
                 out=words[:].bitcast(FP8X4),
                 scales=planes[:],
-                in_=grouped[:].rearrange("q b t -> q (b t)"),
+                in_=h_groups[r][:].rearrange("q b t -> q (b t)"),
             )
+
+        def second_matmul(r):
+            c, e = divmod(r, E)
+            words, planes = h_packed[r]
             y = yps.tile([P, CHUNK, L], F32, name="y")
             y_banks[r] = y
             for j in range(CHUNK):
@@ -281,46 +281,50 @@ def tile_mblfe_pa_t_e_kernel(
 
         def gate_and_store(r):
             c, e = divmod(r, E)
-            if e == 0:
-                out_tile = obp.tile([P, CHUNK, E, L], F32, name="out_tile")
-                out_tiles[c] = out_tile
+            out_tile = obp.tile([P, CHUNK, L], F32, name="out_tile")
             nc.vector.tensor_tensor(
-                out=out_tiles[c][:, :, e, :],
-                in0=y_biased[r][:],
-                in1=by_expert(gates)[:, CHUNK * c : CHUNK * (c + 1), e].unsqueeze(2).to_broadcast([P, CHUNK, L]),
+                out=out_tile[:, 0:VECTOR_TILES, :],
+                in0=y_biased[r][:, 0:VECTOR_TILES, :],
+                in1=by_expert(gates)[:, CHUNK * c : CHUNK * c + VECTOR_TILES, e]
+                .unsqueeze(2)
+                .to_broadcast([P, VECTOR_TILES, L]),
                 op=ALU.mult,
             )
-            if e == E - 1:
-                queue = nc.sync if c == CHUNKS - 1 else nc.gpsimd
-                queue.dma_start(
-                    out=out_rows[:, CHUNK * c : CHUNK * (c + 1), :],
-                    in_=out_tiles[c][:].rearrange("p j e l -> p j (e l)"),
+            for j in range(VECTOR_TILES, CHUNK):
+                col = E * (CHUNK * c + j) + e
+                nc.scalar.activation(
+                    out=out_tile[:, j, :], in_=y_biased[r][:, j, :], func=ACT.Copy, scale=gates[:, col : col + 1]
                 )
+            nc.sync.dma_start(out=out_rows[:, CHUNK * c : CHUNK * (c + 1), L * e : L * (e + 1)], in_=out_tile[:])
 
         with tc.manual_schedule():
-            transpose_x(0)
+            transpose_x(0, 0)
+            transpose_x(0, 1)
             spread_b1()
             sort_w1(0)
-            quantise_x(0)
+            quantise_x(0, 0)
+            quantise_x(0, 1)
             for e in range(1, E):
                 sort_w1(e)
             noisy_logits()
 
-            for r in range(ROUNDS + 6):
+            for r in range(ROUNDS + 7):
                 if r < ROUNDS:
                     hidden(r)
+                if 0 <= r - 5 < ROUNDS:
+                    second_matmul(r - 5)
                 if r == 1:
                     gates_from_logits()
                 if 0 <= r - 3 < ROUNDS:
                     regroup(r - 3)
-                if 0 <= r - 5 < ROUNDS:
-                    add_b2(r - 5)
+                if 0 <= r - 6 < ROUNDS:
+                    add_b2(r - 6)
                 if 0 <= r - 4 < ROUNDS:
-                    second_matmul(r - 4)
-                if 0 <= r - 5 < ROUNDS:
-                    gate_and_store(r - 5)
-                c_next = r // E + 1
-                if c_next < CHUNKS and r % E == 0:
-                    transpose_x(c_next)
-                if c_next < CHUNKS and r % E == 1:
-                    quantise_x(c_next)
+                    quantise_h(r - 4)
+                if 0 <= r - 6 < ROUNDS:
+                    gate_and_store(r - 6)
+                c_next, step = r // E + 1, r % E
+                if c_next < CHUNKS and step < 2:
+                    transpose_x(c_next, step)
+                if c_next < CHUNKS and 1 <= step < 3:
+                    quantise_x(c_next, step - 1)

@@ -53,12 +53,12 @@ def tile_mblfe_pa_t_e_kernel(
         ident = keep.tile([P, P], F32)
         make_identity(nc, ident[:])
 
-        w1_raw = keep.tile([P, E, H], U32, align_bytes=64)
-        w1_planes_raw = keep.tile([P, H], U8, align_bytes=64)
+        w1_words = keep.tile([P, E, H], U32, align_bytes=64)
+        w1_planes = keep.tile([P, H], U8, align_bytes=64)
         w2_words = keep.tile([P, E, L], U32, align_bytes=64)
         w2_planes = keep.tile([P, L], U8, align_bytes=64)
         b1_as_rows = keep.tile([P, P], BF16)
-        nc.vector.memset(w1_planes_raw[:].bitcast(I32), 0)
+        nc.vector.memset(w1_planes[:].bitcast(I32), 0)
         nc.vector.memset(w2_planes[:].bitcast(I32), 0)
         nc.vector.memset(b1_as_rows[:], 0.0)
 
@@ -75,10 +75,10 @@ def tile_mblfe_pa_t_e_kernel(
                 )
 
         nc.sync.dma_start(out=x_chunks[0][:], in_=x_rows[:, 0:CHUNK, :])
-        load_planes(w1_planes_raw, W1_scales)
+        load_planes(w1_planes, W1_scales)
         for e in range(E):
             nc.sync.dma_start(
-                out=w1_raw[:, e, :].bitcast(I32),
+                out=w1_words[:, e, :].bitcast(I32),
                 in_=W1_words[e].rearrange("p n t -> p (n t)").bitcast(I32),
             )
         load_planes(w2_planes, W2_scales)
@@ -90,11 +90,7 @@ def tile_mblfe_pa_t_e_kernel(
         for c in range(1, CHUNKS):
             nc.gpsimd.dma_start(out=x_chunks[c][:], in_=x_rows[:, CHUNK * c : CHUNK * (c + 1), :])
 
-        for e in range(E):
-            nc.scalar.dma_start(
-                out=b1_as_rows[SETS * e : SETS * (e + 1), :].rearrange("s (a i) -> s a i", i=PACK),
-                in_=b1[e].rearrange("(a s i) -> s a i", s=SETS, i=PACK),
-            )
+        nc.scalar.dma_start(out=b1_as_rows[0 : E * SETS, :], in_=b1.rearrange("e (s m) -> (e s) m", m=P))
         pre_in = keep.tile([P, TILES * E], BF16)
         nc.scalar.dma_start(out=pre_in[:], in_=noise_pre.rearrange("(p i) e -> p (i e)", i=TILES))
         noise_in = keep.tile([P, TILES * E], BF16)
@@ -106,19 +102,6 @@ def tile_mblfe_pa_t_e_kernel(
             out=b2_rows[:].rearrange("p e l -> p (e l)"),
             in_=b2.rearrange("e l -> (e l)").partition_broadcast(P),
         )
-
-        w1_words = keep.tile([P, E, SETS, P], U32, align_bytes=64)
-        w1_planes = keep.tile([P, SETS, P], U8, align_bytes=64)
-        nc.vector.tensor_copy(
-            out=w1_planes[:].bitcast(I32),
-            in_=w1_planes_raw[:].bitcast(I32).rearrange("p (a s) -> p s a", s=SETS),
-        )
-
-        def sort_w1(e):
-            nc.vector.tensor_copy(
-                out=w1_words[:, e].bitcast(I32).rearrange("p s (a i) -> p s a i", i=PACK),
-                in_=w1_raw[:, e, :].bitcast(I32).rearrange("p (a s i) -> p s a i", s=SETS, i=PACK),
-            )
 
         x_words = keep.tile([P, B], U32, align_bytes=64)
         x_planes = keep.tile([P, B], U8, align_bytes=64)
@@ -222,8 +205,8 @@ def tile_mblfe_pa_t_e_kernel(
                 z = zps.tile([P, ROWS], F32, name="z")
                 nc.tensor.matmul_mx(
                     out=z[:],
-                    lhsT=w1_words[:, e, s, :].bitcast(FP8X4),
-                    lhsT_scale=w1_planes[4 * e : P, s, :],
+                    lhsT=w1_words[:, e, P * s : P * (s + 1)].bitcast(FP8X4),
+                    lhsT_scale=w1_planes[4 * e : P, P * s : P * (s + 1)],
                     rhs=x_words[:, ROWS * c : ROWS * (c + 1)].bitcast(FP8X4),
                     rhs_scale=x_planes[:, ROWS * c : ROWS * (c + 1)],
                     start=True,
@@ -232,7 +215,7 @@ def tile_mblfe_pa_t_e_kernel(
                 h_set = htp.tile([P, ROWS], BF16, name="h_set")
                 col = SETS * e + s
                 nc.scalar.activation(out=h_set[:], in_=z[:], func=ACT.Tanh, bias=b1_cols[:, col : col + 1])
-                nc.sync.dma_start(out=apart[s:P:SETS, :, :], in_=h_set[:])
+                nc.sync.dma_start(out=apart[32 * s : 32 * (s + 1), :, :], in_=h_set[:])
 
         def regroup(r):
             grouped = hgr.tile([P, ROWS, PACK], BF16, align_bytes=64, name="h_grouped")
@@ -301,11 +284,8 @@ def tile_mblfe_pa_t_e_kernel(
             transpose_x(0, 0)
             transpose_x(0, 1)
             spread_b1()
-            sort_w1(0)
             quantise_x(0, 0)
             quantise_x(0, 1)
-            for e in range(1, E):
-                sort_w1(e)
             noisy_logits()
 
             for r in range(ROUNDS + 7):

@@ -22,7 +22,7 @@ CHUNKS = TILES // CHUNK
 ROWS = CHUNK * P
 ROUNDS = CHUNKS * E
 SETS = H // P
-VECTOR_TILES = 3
+VECTOR_TILES = 2
 NOISE_EPS = 0.01
 MEAN_EPS = 1e-8
 
@@ -53,12 +53,12 @@ def tile_mblfe_pa_t_e_kernel(
         ident = keep.tile([P, P], F32)
         make_identity(nc, ident[:])
 
-        w1_words = keep.tile([P, E, H], U32, align_bytes=64)
-        w1_planes = keep.tile([P, H], U8, align_bytes=64)
+        w1_raw = keep.tile([P, E, H], U32, align_bytes=64)
+        w1_planes_raw = keep.tile([P, H], U8, align_bytes=64)
         w2_words = keep.tile([P, E, L], U32, align_bytes=64)
         w2_planes = keep.tile([P, L], U8, align_bytes=64)
         b1_as_rows = keep.tile([P, P], BF16)
-        nc.vector.memset(w1_planes[:].bitcast(I32), 0)
+        nc.vector.memset(w1_planes_raw[:].bitcast(I32), 0)
         nc.vector.memset(w2_planes[:].bitcast(I32), 0)
         nc.vector.memset(b1_as_rows[:], 0.0)
 
@@ -75,10 +75,10 @@ def tile_mblfe_pa_t_e_kernel(
                 )
 
         nc.sync.dma_start(out=x_chunks[0][:], in_=x_rows[:, 0:CHUNK, :])
-        load_planes(w1_planes, W1_scales)
+        load_planes(w1_planes_raw, W1_scales)
         for e in range(E):
             nc.sync.dma_start(
-                out=w1_words[:, e, :].bitcast(I32),
+                out=w1_raw[:, e, :].bitcast(I32),
                 in_=W1_words[e].rearrange("p n t -> p (n t)").bitcast(I32),
             )
         load_planes(w2_planes, W2_scales)
@@ -90,7 +90,11 @@ def tile_mblfe_pa_t_e_kernel(
         for c in range(1, CHUNKS):
             nc.gpsimd.dma_start(out=x_chunks[c][:], in_=x_rows[:, CHUNK * c : CHUNK * (c + 1), :])
 
-        nc.scalar.dma_start(out=b1_as_rows[0 : E * SETS, :], in_=b1.rearrange("e (s m) -> (e s) m", m=P))
+        for e in range(E):
+            nc.scalar.dma_start(
+                out=b1_as_rows[SETS * e : SETS * (e + 1), :].rearrange("s (a i) -> s a i", i=PACK),
+                in_=b1[e].rearrange("(a s i) -> s a i", s=SETS, i=PACK),
+            )
         pre_in = keep.tile([P, TILES * E], BF16)
         nc.scalar.dma_start(out=pre_in[:], in_=noise_pre.rearrange("(p i) e -> p (i e)", i=TILES))
         noise_in = keep.tile([P, TILES * E], BF16)
@@ -102,6 +106,19 @@ def tile_mblfe_pa_t_e_kernel(
             out=b2_rows[:].rearrange("p e l -> p (e l)"),
             in_=b2.rearrange("e l -> (e l)").partition_broadcast(P),
         )
+
+        w1_words = keep.tile([P, E, SETS, P], U32, align_bytes=64)
+        w1_planes = keep.tile([P, SETS, P], U8, align_bytes=64)
+        nc.vector.tensor_copy(
+            out=w1_planes[:].bitcast(I32),
+            in_=w1_planes_raw[:].bitcast(I32).rearrange("p (a s) -> p s a", s=SETS),
+        )
+
+        def sort_w1(e):
+            nc.vector.tensor_copy(
+                out=w1_words[:, e].bitcast(I32).rearrange("p s (a i) -> p s a i", i=PACK),
+                in_=w1_raw[:, e, :].bitcast(I32).rearrange("p (a s i) -> p s a i", s=SETS, i=PACK),
+            )
 
         x_words = keep.tile([P, B], U32, align_bytes=64)
         x_planes = keep.tile([P, B], U8, align_bytes=64)
@@ -205,8 +222,8 @@ def tile_mblfe_pa_t_e_kernel(
                 z = zps.tile([P, ROWS], F32, name="z")
                 nc.tensor.matmul_mx(
                     out=z[:],
-                    lhsT=w1_words[:, e, P * s : P * (s + 1)].bitcast(FP8X4),
-                    lhsT_scale=w1_planes[4 * e : P, P * s : P * (s + 1)],
+                    lhsT=w1_words[:, e, s, :].bitcast(FP8X4),
+                    lhsT_scale=w1_planes[4 * e : P, s, :],
                     rhs=x_words[:, ROWS * c : ROWS * (c + 1)].bitcast(FP8X4),
                     rhs_scale=x_planes[:, ROWS * c : ROWS * (c + 1)],
                     start=True,
@@ -215,7 +232,7 @@ def tile_mblfe_pa_t_e_kernel(
                 h_set = htp.tile([P, ROWS], BF16, name="h_set")
                 col = SETS * e + s
                 nc.scalar.activation(out=h_set[:], in_=z[:], func=ACT.Tanh, bias=b1_cols[:, col : col + 1])
-                nc.sync.dma_start(out=apart[32 * s : 32 * (s + 1), :, :], in_=h_set[:])
+                nc.sync.dma_start(out=apart[s:P:SETS, :, :], in_=h_set[:])
 
         def regroup(r):
             grouped = hgr.tile([P, ROWS, PACK], BF16, align_bytes=64, name="h_grouped")
@@ -284,8 +301,11 @@ def tile_mblfe_pa_t_e_kernel(
             transpose_x(0, 0)
             transpose_x(0, 1)
             spread_b1()
+            sort_w1(0)
             quantise_x(0, 0)
             quantise_x(0, 1)
+            for e in range(1, E):
+                sort_w1(e)
             noisy_logits()
 
             for r in range(ROUNDS + 7):

from contextlib import ExitStack

import concourse.mybir as mybir
from concourse.masks import make_identity

FP8X4 = mybir.dt.float8_e4m3fn_x4
BF16 = mybir.dt.bfloat16
F32 = mybir.dt.float32
I32 = mybir.dt.int32
U32 = mybir.dt.uint32
U8 = mybir.dt.uint8
ACT = mybir.ActivationFunctionType
ALU = mybir.AluOpType
AX = mybir.AxisListType

P = 128
PACK = 4
B, D, E, H, L = 4096, 512, 4, 512, 128
TILES = B // P
CHUNK = 4
CHUNKS = TILES // CHUNK
ROWS = CHUNK * P
ROUNDS = CHUNKS * E
SETS = H // P
VECTOR_TILES = 2
NOISE_EPS = 0.01
MEAN_EPS = 1e-8

FLOPS = 2 * B * E * (D * H + H * L)


def tile_mblfe_pa_t_e_kernel(
    tc, x, noise, clean_logits, noise_pre, W1_words, W1_scales, b1, W2_words, W2_scales, b2, out
):
    nc = tc.nc
    with ExitStack() as ctx:
        keep = ctx.enter_context(tc.tile_pool(name="keep", bufs=1))
        xin = ctx.enter_context(tc.tile_pool(name="xin", bufs=CHUNKS))
        xgr = ctx.enter_context(tc.tile_pool(name="xgr", bufs=3))
        htp = ctx.enter_context(tc.tile_pool(name="htp", bufs=12))
        plp = ctx.enter_context(tc.tile_pool(name="plp", bufs=6))
        hgr = ctx.enter_context(tc.tile_pool(name="hgr", bufs=3))
        hq = ctx.enter_context(tc.tile_pool(name="hq", bufs=3))
        ybp = ctx.enter_context(tc.tile_pool(name="ybp", bufs=2))
        obp = ctx.enter_context(tc.tile_pool(name="obp", bufs=4))
        zps = ctx.enter_context(tc.psum_pool(name="zps", bufs=4))
        trp = ctx.enter_context(tc.psum_pool(name="trp", bufs=2))
        yps = ctx.enter_context(tc.psum_pool(name="yps", bufs=2))

        x_rows = x.rearrange("(p i) d -> p i d", i=TILES)
        out_rows = out.rearrange("(p i) e l -> p i (e l)", i=TILES)

        ident = keep.tile([P, P], F32)
        make_identity(nc, ident[:])

        w1_raw = keep.tile([P, E, H], U32, align_bytes=64)
        w1_planes_raw = keep.tile([P, H], U8, align_bytes=64)
        w2_words = keep.tile([P, E, L], U32, align_bytes=64)
        w2_planes = keep.tile([P, L], U8, align_bytes=64)
        b1_as_rows = keep.tile([P, P], BF16)
        nc.vector.memset(w1_planes_raw[:].bitcast(I32), 0)
        nc.vector.memset(w2_planes[:].bitcast(I32), 0)
        nc.vector.memset(b1_as_rows[:], 0.0)

        x_chunks = []
        for c in range(CHUNKS):
            x_chunk = xin.tile([P, CHUNK, D], BF16, name="x_chunk")
            x_chunks.append(x_chunk)

        def load_planes(planes, scales):
            for quad in range(4):
                nc.sync.dma_start(
                    out=planes[32 * quad : 32 * quad + 16, :].bitcast(I32),
                    in_=scales[:, 4 * quad : 4 * quad + 4, :].bitcast(I32),
                )

        nc.sync.dma_start(out=x_chunks[0][:], in_=x_rows[:, 0:CHUNK, :])
        load_planes(w1_planes_raw, W1_scales)
        for e in range(E):
            nc.sync.dma_start(
                out=w1_raw[:, e, :].bitcast(I32),
                in_=W1_words[e].rearrange("p n t -> p (n t)").bitcast(I32),
            )
        load_planes(w2_planes, W2_scales)
        for e in range(E):
            nc.sync.dma_start(
                out=w2_words[:, e, :].bitcast(I32),
                in_=W2_words[e].rearrange("p n t -> p (n t)").bitcast(I32),
            )
        for c in range(1, CHUNKS):
            nc.gpsimd.dma_start(out=x_chunks[c][:], in_=x_rows[:, CHUNK * c : CHUNK * (c + 1), :])

        for e in range(E):
            nc.scalar.dma_start(
                out=b1_as_rows[SETS * e : SETS * (e + 1), :].rearrange("s (a i) -> s a i", i=PACK),
                in_=b1[e].rearrange("(a s i) -> s a i", s=SETS, i=PACK),
            )
        pre_in = keep.tile([P, TILES * E], BF16)
        nc.scalar.dma_start(out=pre_in[:], in_=noise_pre.rearrange("(p i) e -> p (i e)", i=TILES))
        noise_in = keep.tile([P, TILES * E], BF16)
        nc.scalar.dma_start(out=noise_in[:], in_=noise.rearrange("(p i) e -> p (i e)", i=TILES))
        clean_in = keep.tile([P, TILES * E], BF16)
        nc.scalar.dma_start(out=clean_in[:], in_=clean_logits.rearrange("(p i) e -> p (i e)", i=TILES))
        b2_rows = keep.tile([P, E, L], BF16)
        nc.scalar.dma_start(
            out=b2_rows[:].rearrange("p e l -> p (e l)"),
            in_=b2.rearrange("e l -> (e l)").partition_broadcast(P),
        )

        w1_words = keep.tile([P, E, SETS, P], U32, align_bytes=64)
        w1_planes = keep.tile([P, SETS, P], U8, align_bytes=64)
        nc.vector.tensor_copy(
            out=w1_planes[:].bitcast(I32),
            in_=w1_planes_raw[:].bitcast(I32).rearrange("p (a s) -> p s a", s=SETS),
        )

        def sort_w1(e):
            nc.vector.tensor_copy(
                out=w1_words[:, e].bitcast(I32).rearrange("p s (a i) -> p s a i", i=PACK),
                in_=w1_raw[:, e, :].bitcast(I32).rearrange("p (a s i) -> p s a i", s=SETS, i=PACK),
            )

        x_words = keep.tile([P, B], U32, align_bytes=64)
        x_planes = keep.tile([P, B], U8, align_bytes=64)
        x_groups = {}

        def transpose_x(c, half):
            grouped = xgr.tile([P, 2, P, PACK], BF16, align_bytes=64, name="x_grouped")
            x_groups[(c, half)] = grouped
            turned = trp.tile([P, 2, 2, P], F32, name="x_turned")
            for j in range(2):
                row_words = x_chunks[c][:, 2 * half + j, :].bitcast(F32)
                for u in range(2):
                    nc.tensor.transpose(turned[:, j, u, :], row_words[:, u : D // 2 : 2], ident[:])
            nc.scalar.copy(out=grouped[:].bitcast(F32), in_=turned[:].rearrange("q j u b -> q j b u"))

        def quantise_x(c, half):
            first = ROWS * c + 2 * P * half
            cols = slice(first, first + 2 * P)
            nc.vector.quantize_mx(
                out=x_words[:, cols].bitcast(FP8X4),
                scales=x_planes[:, cols],
                in_=x_groups[(c, half)][:].rearrange("q j b t -> q (j b t)"),
            )

        b1_cols = keep.tile([P, P], F32)

        def spread_b1():
            b1_wide = keep.tile([P, P], F32, name="b1_wide")
            nc.vector.tensor_copy(out=b1_wide[:], in_=b1_as_rows[:])
            b1_turned = trp.tile([P, P], F32, name="b1_turned", tag="x_turned")
            nc.tensor.transpose(b1_turned[:], b1_wide[:], ident[:])
            nc.vector.tensor_copy(out=b1_cols[:], in_=b1_turned[:])

        def small(name, width=TILES * E):
            return keep.tile([P, width], F32, name=name)

        def by_expert(t):
            return t[:].rearrange("p (i e) -> p i e", e=E)

        def over_experts(t):
            return t[:].unsqueeze(2).to_broadcast([P, TILES, E])

        gates = small("gates")
        logit = small("logit")

        def noisy_logits():
            mag = small("mag")
            nc.scalar.activation(out=mag[:], in_=pre_in[:], func=ACT.Abs)
            nc.scalar.activation(out=mag[:], in_=mag[:], func=ACT.Exp, scale=-1.0)
            nc.scalar.activation(out=mag[:], in_=mag[:], func=ACT.Ln, bias=1.0)
            pos = small("pos")
            nc.vector.tensor_scalar_max(out=pos[:], in0=pre_in[:], scalar1=0.0)
            nc.vector.scalar_tensor_tensor(
                out=logit[:], in0=mag[:], scalar=NOISE_EPS, in1=pos[:], op0=ALU.add, op1=ALU.add
            )
            nc.vector.tensor_tensor(out=logit[:], in0=logit[:], in1=noise_in[:], op=ALU.mult)
            nc.vector.tensor_tensor(out=logit[:], in0=logit[:], in1=clean_in[:], op=ALU.add)
            top = small("top", TILES)
            nc.vector.tensor_reduce(out=top[:], in_=by_expert(logit), axis=AX.X, op=ALU.max)
            nc.vector.tensor_tensor(
                out=by_expert(logit), in0=by_expert(logit), in1=over_experts(top), op=ALU.subtract
            )

        def gates_from_logits():
            prob = small("prob")
            nc.scalar.activation(out=prob[:], in_=logit[:], func=ACT.Exp)
            total = small("total", TILES)
            nc.vector.tensor_reduce(out=total[:], in_=by_expert(prob), axis=AX.X, op=ALU.add)
            nc.vector.reciprocal(out=total[:], in_=total[:])
            nc.vector.tensor_tensor(
                out=by_expert(prob), in0=by_expert(prob), in1=over_experts(total), op=ALU.mult
            )
            cut = small("cut", TILES)
            nc.vector.tensor_reduce(out=cut[:], in_=by_expert(prob), axis=AX.X, op=ALU.add)
            nc.vector.tensor_scalar(
                out=cut[:], in0=cut[:], scalar1=1.0 / E, scalar2=MEAN_EPS, op0=ALU.mult, op1=ALU.subtract
            )
            kept = small("kept")
            nc.vector.tensor_tensor(
                out=by_expert(kept), in0=by_expert(prob), in1=over_experts(cut), op=ALU.is_ge
            )
            nc.vector.tensor_tensor(out=kept[:], in0=kept[:], in1=prob[:], op=ALU.mult)
            kept_sum = small("kept_sum", TILES)
            nc.vector.tensor_reduce(out=kept_sum[:], in_=by_expert(kept), axis=AX.X, op=ALU.add)
            nc.vector.reciprocal(out=kept_sum[:], in_=kept_sum[:])
            nc.vector.tensor_tensor(
                out=by_expert(gates), in0=by_expert(kept), in1=over_experts(kept_sum), op=ALU.mult
            )

        h_planes_of = {}
        h_groups = {}
        h_packed = {}
        y_banks = {}
        y_biased = {}

        def hidden(r):
            c, e = divmod(r, E)
            apart = plp.tile([P, PACK, ROWS], BF16, name="h_apart")
            h_planes_of[r] = apart
            for s in range(SETS):
                z = zps.tile([P, ROWS], F32, name="z")
                nc.tensor.matmul_mx(
                    out=z[:],
                    lhsT=w1_words[:, e, s, :].bitcast(FP8X4),
                    lhsT_scale=w1_planes[4 * e : P, s, :],
                    rhs=x_words[:, ROWS * c : ROWS * (c + 1)].bitcast(FP8X4),
                    rhs_scale=x_planes[:, ROWS * c : ROWS * (c + 1)],
                    start=True,
                    stop=True,
                )
                h_set = htp.tile([P, ROWS], BF16, name="h_set")
                col = SETS * e + s
                nc.scalar.activation(out=h_set[:], in_=z[:], func=ACT.Tanh, bias=b1_cols[:, col : col + 1])
                nc.sync.dma_start(out=apart[s:P:SETS, :, :], in_=h_set[:])

        def regroup(r):
            grouped = hgr.tile([P, ROWS, PACK], BF16, align_bytes=64, name="h_grouped")
            h_groups[r] = grouped
            nc.vector.tensor_copy(
                out=grouped[:].rearrange("q (g i) t -> q g t i", i=4),
                in_=h_planes_of[r][:].rearrange("q t (g i) -> q g t i", i=4),
            )

        def quantise_h(r):
            words = hq.tile([P, ROWS], U32, align_bytes=64, name="h_words")
            planes = hq.tile([P, ROWS], U8, align_bytes=64, name="h_planes")
            h_packed[r] = (words, planes)
            nc.vector.quantize_mx(
                out=words[:].bitcast(FP8X4),
                scales=planes[:],
                in_=h_groups[r][:].rearrange("q b t -> q (b t)"),
            )

        def second_matmul(r):
            c, e = divmod(r, E)
            words, planes = h_packed[r]
            y = yps.tile([P, CHUNK, L], F32, name="y")
            y_banks[r] = y
            for j in range(CHUNK):
                nc.tensor.matmul_mx(
                    out=y[:, j, :],
                    lhsT=words[:, P * j : P * (j + 1)].bitcast(FP8X4),
                    lhsT_scale=planes[:, P * j : P * (j + 1)],
                    rhs=w2_words[:, e, :].bitcast(FP8X4),
                    rhs_scale=w2_planes[4 * e : P, :],
                    start=True,
                    stop=True,
                )

        def add_b2(r):
            c, e = divmod(r, E)
            yb = ybp.tile([P, CHUNK, L], F32, name="yb")
            y_biased[r] = yb
            nc.vector.tensor_tensor(
                out=yb[:],
                in0=y_banks[r][:],
                in1=b2_rows[:, e, :].unsqueeze(1).to_broadcast([P, CHUNK, L]),
                op=ALU.add,
            )

        def gate_and_store(r):
            c, e = divmod(r, E)
            out_tile = obp.tile([P, CHUNK, L], F32, name="out_tile")
            nc.vector.tensor_tensor(
                out=out_tile[:, 0:VECTOR_TILES, :],
                in0=y_biased[r][:, 0:VECTOR_TILES, :],
                in1=by_expert(gates)[:, CHUNK * c : CHUNK * c + VECTOR_TILES, e]
                .unsqueeze(2)
                .to_broadcast([P, VECTOR_TILES, L]),
                op=ALU.mult,
            )
            for j in range(VECTOR_TILES, CHUNK):
                col = E * (CHUNK * c + j) + e
                nc.scalar.activation(
                    out=out_tile[:, j, :], in_=y_biased[r][:, j, :], func=ACT.Copy, scale=gates[:, col : col + 1]
                )
            nc.sync.dma_start(out=out_rows[:, CHUNK * c : CHUNK * (c + 1), L * e : L * (e + 1)], in_=out_tile[:])

        with tc.manual_schedule():
            transpose_x(0, 0)
            transpose_x(0, 1)
            spread_b1()
            sort_w1(0)
            quantise_x(0, 0)
            quantise_x(0, 1)
            for e in range(1, E):
                sort_w1(e)
            noisy_logits()

            for r in range(ROUNDS + 7):
                if r < ROUNDS:
                    hidden(r)
                if 0 <= r - 5 < ROUNDS:
                    second_matmul(r - 5)
                if r == 1:
                    gates_from_logits()
                if 0 <= r - 3 < ROUNDS:
                    regroup(r - 3)
                if 0 <= r - 6 < ROUNDS:
                    add_b2(r - 6)
                if 0 <= r - 4 < ROUNDS:
                    quantise_h(r - 4)
                if 0 <= r - 6 < ROUNDS:
                    gate_and_store(r - 6)
                c_next, step = r // E + 1, r % E
                if c_next < CHUNKS and step < 2:
                    transpose_x(c_next, step)
                if c_next < CHUNKS and 1 <= step < 3:
                    quantise_x(c_next, step - 1)
